import numpy as np
import ml_dtypes


def mxq(x, axis, fmt="e4m3"):
    dtype, down = {"e4m3": (ml_dtypes.float8_e4m3fn, 7), "e5m2": (ml_dtypes.float8_e5m2, 14)}[fmt]
    v = np.moveaxis(np.asarray(x, np.float32).astype(ml_dtypes.bfloat16).astype(np.float64), axis, -1)
    blocks = v.reshape(v.shape[:-1] + (-1, 32))
    amax = np.abs(blocks).max(-1, keepdims=True)
    byte = np.maximum(np.where(amax > 0, np.frexp(amax)[1] - 1 + 127, 0) - down, 1)
    scale = np.exp2(byte - 127.0)
    codes = (blocks / scale).astype(np.float32).astype(dtype).astype(np.float64)
    return np.moveaxis((codes * scale).reshape(v.shape), -1, axis)


WIDE = False


def mx_kscale(k):
    if not WIDE:
        return np.ones(k)
    levels = np.array([10, -10, 5, -5, 0])
    a = np.random.permutation(np.resize(levels, k // 512 * 4)).reshape(k // 512, 4)
    idx = np.arange(k)
    return np.exp2(a[idx // 512, idx % 128 // 32])


BF16 = ml_dtypes.bfloat16


def bf(x):
    return np.asarray(x, np.float32).astype(BF16)


def f64(x):
    return np.asarray(x).astype(np.float64)


B, S, HID, H, HKV, DH = 4, 2048, 512, 2, 1, 64
NH = H + 2 * HKV


def rotate_half(x):
    x1 = x[..., ::2]
    x2 = x[..., 1::2]
    return np.stack((-x2, x1), axis=-1).reshape(x.shape)


def setup_inputs():
    s = mx_kscale(HID)
    inv_freq = 1.0 / (10000.0 ** (np.arange(0, DH, 2) / DH))
    emb = np.repeat(np.outer(np.arange(S), inv_freq), 2, axis=-1)
    return {"hidden_states": bf(np.random.standard_normal((B, S, HID)) * s),
            "cos": bf(np.cos(emb)),
            "sin": bf(np.sin(emb)),
            "w_qkv": bf(np.random.standard_normal((NH * DH, HID)) / np.sqrt(HID) / s[None, :])}


def reference(hidden_states, cos, sin, w_qkv):
    qkv = mxq(f64(hidden_states), 2, "e4m3") @ mxq(f64(w_qkv), 1, "e4m3").T
    qkv = qkv.reshape(B, S, NH, DH)
    q = qkv[:, :, :H]
    k = qkv[:, :, H:H + HKV]
    v = qkv[:, :, H + HKV:]
    cos_s = f64(cos)[:S][None, :, None, :]
    sin_s = f64(sin)[:S][None, :, None, :]
    q = q * cos_s + rotate_half(q) * sin_s
    k = k * cos_s + rotate_half(k) * sin_s
    return q, k, v

@@ -1,0 +1,205 @@
+from contextlib import ExitStack
+
+import concourse.mybir as mybir
+from concourse.masks import make_identity
+
+F32 = mybir.dt.float32
+BF16 = mybir.dt.bfloat16
+U32 = mybir.dt.uint32
+U8 = mybir.dt.uint8
+FP8X4 = mybir.dt.float8_e4m3fn_x4
+MULT = mybir.AluOpType.mult
+ADD = mybir.AluOpType.add
+
+P = 128
+B, S, HID = 4, 2048, 512
+DH = 64
+TPB = S // P
+GT = 4
+NG = B * TPB // GT
+FLOPS = 2 * B * S * HID * 256
+
+LOADS = [(0, 0, 4), (0, 4, 4), (0, 8, 8), (1, 0, 16), (2, 0, 16), (3, 0, 16)]
+STORES = [(0, 0, 8), (0, 8, 8), (1, 0, 8), (1, 8, 8), (2, 0, 8), (2, 8, 8), (3, 0, 8), (3, 8, 4), (3, 12, 4)]
+V_ADD_Q = (15,)
+V_ADD_K = (15,)
+
+
+def tile_attention_pa_t_kernel(tc, hidden_states, cos, sin, w_qkv, out_0, out_1, out_2):
+    nc = tc.nc
+    with ExitStack() as ctx:
+        const = ctx.enter_context(tc.tile_pool(name="const", bufs=1))
+        xin = ctx.enter_context(tc.tile_pool(name="xin", bufs=1))
+        outp = ctx.enter_context(tc.tile_pool(name="outp", bufs=1))
+        gp = ctx.enter_context(tc.tile_pool(name="gp", bufs=3))
+        cp = ctx.enter_context(tc.tile_pool(name="cp", bufs=2))
+        pp = ctx.enter_context(tc.tile_pool(name="pp", bufs=3))
+        tpp = ctx.enter_context(tc.psum_pool(name="tpp", bufs=4))
+        mmp = ctx.enter_context(tc.psum_pool(name="mmp", bufs=4))
+        ctx.enter_context(tc.manual_schedule())
+
+        ident = const.tile([P, P], F32, name="ident")
+        make_identity(nc, ident[:])
+        perm = const.tile([P, P], F32, name="perm")
+        w_sb = const.tile([P, 2, HID], BF16, name="w_sb")
+        tab = const.tile([P, 2, TPB, DH], BF16, name="tab")
+
+        nc.sync.dma_start(out=w_sb[:], in_=w_qkv.rearrange("(a p) k -> p a k", p=P))
+        x_of = {}
+        x_tiles = []
+        for (b, t0, n) in LOADS:
+            xt = xin.tile([P, n, HID], BF16, name="x%d_%d" % (b, t0))
+            x_tiles.append((xt, b, t0, n))
+            for l0 in range(0, n, GT):
+                x_of[(b * TPB + t0 + l0) // GT] = (xt, l0)
+
+        def load_x(i):
+            xt, b, t0, n = x_tiles[i]
+            nc.sync.dma_start(
+                out=xt[:],
+                in_=hidden_states[b].rearrange("(p t) k -> p t k", t=TPB)[:, t0:t0 + n, :],
+            )
+
+        load_x(0)
+        load_x(1)
+        nc.sync.dma_start(out=tab[:, 1], in_=sin.rearrange("(p t) j -> p t j", t=TPB))
+        nc.sync.dma_start(out=tab[:, 0], in_=cos.rearrange("(p t) j -> p t j", t=TPB))
+        for i in range(2, len(LOADS)):
+            load_x(i)
+
+        out_of = {}
+        for (b, t0, n) in STORES:
+            q_sb = outp.tile([P, n, 2 * DH], F32, name="q%d_%d" % (b, t0))
+            k_sb = outp.tile([P, n, DH], F32, name="k%d_%d" % (b, t0))
+            v_sb = outp.tile([P, n, DH], F32, name="v%d_%d" % (b, t0))
+            for l0 in range(0, n, GT):
+                out_of[(b * TPB + t0 + l0) // GT] = (q_sb, k_sb, v_sb, l0, l0 + GT == n, b, t0, n)
+
+        iv = ident[:].rearrange("p (n e) -> p n e", e=2)
+        pv = perm[:].rearrange("p (n e) -> p n e", e=2)
+        nc.vector.tensor_copy(out=pv[:, :, 0], in_=iv[:, :, 1])
+        nc.vector.tensor_copy(out=pv[:, :, 1], in_=iv[:, :, 0])
+
+        def evac(eng_is_vector, dst, bank):
+            src = bank[:].rearrange("p a u r -> p a r u")
+            if eng_is_vector:
+                nc.vector.tensor_copy(out=dst, in_=src)
+            else:
+                nc.scalar.copy(out=dst, in_=src)
+
+        banks_of = {}
+        grp_of = {}
+        code_of = {}
+        mm_of = {}
+        p_of = {}
+
+        def stage_t(g):
+            xt, l0 = x_of[g]
+            xw = xt[:].bitcast(F32)
+            banks = []
+            for h in range(2):
+                tp = tpp.tile([P, 2, 2, P], F32, name="tp", tag="tp")
+                for a in range(2):
+                    for u in range(2):
+                        nc.tensor.transpose(tp[:, a, u, :], xw[:, l0 + 2 * h + a, P * u:P * (u + 1)], ident[:])
+                banks.append(tp)
+            banks_of[g] = banks
+
+        def stage_e(g, second_on_vector=False):
+            grp = gp.tile([P, GT, P, 4], BF16, name="grp", tag="grp", align_bytes=64)
+            banks = banks_of[g]
+            evac(False, grp[:, 0:2].bitcast(F32), banks[0])
+            evac(second_on_vector, grp[:, 2:4].bitcast(F32), banks[1])
+            grp_of[g] = grp
+
+        def stage_q(g):
+            codes = cp.tile([P, GT * P], U32, name="codes", tag="codes", align_bytes=64)
+            scl = cp.tile([P, GT * P], U8, name="scl", tag="scl", align_bytes=64)
+            nc.vector.quantize_mx(
+                out=codes[:].bitcast(FP8X4),
+                scales=scl[:],
+                in_=grp_of[g][:].rearrange("p a r t -> p (a r t)"),
+            )
+            code_of[g] = (codes, scl)
+
+        def stage_m(g, i):
+            codes, scl = code_of[g]
+            mm = mmp.tile([P, 512], F32, name="mm", tag="mm")
+            nc.tensor.matmul_mx(
+                out=mm[:],
+                lhsT=codes[:, P * i:P * (i + 1)].bitcast(FP8X4),
+                lhsT_scale=scl[:, P * i:P * (i + 1)],
+                rhs=w_codes[:].bitcast(FP8X4),
+                rhs_scale=w_scl[:],
+                start=True,
+                stop=True,
+            )
+            mm_of[(g, i)] = mm
+            v_sb, l0 = out_of[g][2], out_of[g][3]
+            nc.scalar.copy(out=v_sb[:, l0 + i, :], in_=mm[:, 3 * DH:4 * DH])
+
+        def stage_x(g, i):
+            if i == 0:
+                p_of[g] = pp.tile([P, GT, 2, 3 * DH], F32, name="prod", tag="prod")
+            t = (g * GT + i) % TPB
+            nc.vector.tensor_tensor(
+                out=p_of[g][:, i].rearrange("p c (h j) -> p c h j", h=3),
+                in0=mm_of[(g, i)][:].rearrange("p (c h j) -> p c h j", c=2, h=4)[:, :, 0:3, :],
+                in1=tab[:, :, t, :].unsqueeze(2).to_broadcast([P, 2, 3, DH]),
+                op=MULT,
+            )
+
+        def stage_a(g):
+            q_sb, k_sb, v_sb, l0, last, b, t0, n = out_of[g]
+            prod = p_of[g]
+            eq = nc.vector if g in V_ADD_Q else nc.gpsimd
+            ek = nc.vector if g in V_ADD_K else nc.gpsimd
+            eq.tensor_tensor(out=q_sb[:, l0:l0 + GT, :], in0=prod[:, :, 0, 0:2 * DH], in1=prod[:, :, 1, 0:2 * DH], op=ADD)
+            ek.tensor_tensor(out=k_sb[:, l0:l0 + GT, :], in0=prod[:, :, 0, 2 * DH:3 * DH], in1=prod[:, :, 1, 2 * DH:3 * DH], op=ADD)
+            if last:
+                nc.sync.dma_start(out=out_2[b].rearrange("(p t) h j -> p t (h j)", t=TPB)[:, t0:t0 + n, :], in_=v_sb[:])
+                nc.sync.dma_start(out=out_0[b].rearrange("(p t) h j -> p t (h j)", t=TPB)[:, t0:t0 + n, :], in_=q_sb[:])
+                nc.sync.dma_start(out=out_1[b].rearrange("(p t) h j -> p t (h j)", t=TPB)[:, t0:t0 + n, :], in_=k_sb[:])
+
+        ww = w_sb[:].bitcast(F32)
+        w_grp = const.tile([P, 4, P, 4], BF16, name="w_grp", align_bytes=64)
+        w_codes = const.tile([P, 512], U32, name="w_codes", align_bytes=64)
+        w_scl = const.tile([P, 512], U8, name="w_scl", align_bytes=64)
+        w_banks = []
+        for mat in (ident, perm):
+            tp = tpp.tile([P, 2, 2, P], F32, name="tp", tag="tp")
+            for a in range(2):
+                for u in range(2):
+                    nc.tensor.transpose(tp[:, a, u, :], ww[:, a, P * u:P * (u + 1)], mat[:])
+            w_banks.append(tp)
+        evac(False, w_grp[:, 0:2].bitcast(F32), w_banks[0])
+        evac(True, w_grp[:, 2:4].bitcast(F32), w_banks[1])
+        stage_t(0)
+        nc.vector.quantize_mx(
+            out=w_codes[:].bitcast(FP8X4),
+            scales=w_scl[:],
+            in_=w_grp[:].rearrange("p a r t -> p (a r t)"),
+        )
+        stage_e(0, second_on_vector=True)
+        stage_t(1)
+        stage_q(0)
+        stage_e(1)
+        sv = tab[:, 1].rearrange("p t (i e) -> p (t i) e", e=2)[:, :, 0]
+        nc.vector.tensor_scalar_mul(out=sv, in0=sv, scalar1=-1.0)
+        for i in range(GT):
+            stage_m(0, i)
+        stage_t(2)
+        stage_e(2)
+
+        for k in range(NG):
+            if k + 3 < NG:
+                stage_t(k + 3)
+            if k + 1 < NG:
+                stage_q(k + 1)
+            if k + 3 < NG:
+                stage_e(k + 3)
+            for i in range(GT):
+                stage_x(k, i)
+                if k + 1 < NG:
+                    stage_m(k + 1, i)
+            stage_a(k)

@@ -15,14 +15,12 @@ P = 128
 B, S, HID = 4, 2048, 512
 DH = 64
 TPB = S // P
-GT = 4
-NG = B * TPB // GT
 FLOPS = 2 * B * S * HID * 256
 
 LOADS = [(0, 0, 4), (0, 4, 4), (0, 8, 8), (1, 0, 16), (2, 0, 16), (3, 0, 16)]
-STORES = [(0, 0, 8), (0, 8, 8), (1, 0, 8), (1, 8, 8), (2, 0, 8), (2, 8, 8), (3, 0, 8), (3, 8, 4), (3, 12, 4)]
-V_ADD_Q = (15,)
-V_ADD_K = (15,)
+BLOCKS = [(0, 0, 4), (0, 4, 4), (0, 8, 8), (1, 0, 8), (1, 8, 8), (2, 0, 8), (2, 8, 8), (3, 0, 8), (3, 8, 4), (3, 12, 4)]
+NB = len(BLOCKS)
+AHEAD = 4
 
 
 def tile_attention_pa_t_kernel(tc, hidden_states, cos, sin, w_qkv, out_0, out_1, out_2):
@@ -31,11 +29,11 @@ def tile_attention_pa_t_kernel(tc, hidden_states, cos, sin, w_qkv, out_0, out_1,
         const = ctx.enter_context(tc.tile_pool(name="const", bufs=1))
         xin = ctx.enter_context(tc.tile_pool(name="xin", bufs=1))
         outp = ctx.enter_context(tc.tile_pool(name="outp", bufs=1))
-        gp = ctx.enter_context(tc.tile_pool(name="gp", bufs=3))
+        gp = ctx.enter_context(tc.tile_pool(name="gp", bufs=2))
         cp = ctx.enter_context(tc.tile_pool(name="cp", bufs=2))
         pp = ctx.enter_context(tc.tile_pool(name="pp", bufs=3))
         tpp = ctx.enter_context(tc.psum_pool(name="tpp", bufs=4))
-        mmp = ctx.enter_context(tc.psum_pool(name="mmp", bufs=4))
+        mmp = ctx.enter_context(tc.psum_pool(name="mmp", bufs=AHEAD))
         ctx.enter_context(tc.manual_schedule())
 
         ident = const.tile([P, P], F32, name="ident")
@@ -50,8 +48,8 @@ def tile_attention_pa_t_kernel(tc, hidden_states, cos, sin, w_qkv, out_0, out_1,
         for (b, t0, n) in LOADS:
             xt = xin.tile([P, n, HID], BF16, name="x%d_%d" % (b, t0))
             x_tiles.append((xt, b, t0, n))
-            for l0 in range(0, n, GT):
-                x_of[(b * TPB + t0 + l0) // GT] = (xt, l0)
+            for l in range(n):
+                x_of[(b, t0 + l)] = (xt, l)
 
         def load_x(i):
             xt, b, t0, n = x_tiles[i]
@@ -67,22 +65,25 @@ def tile_attention_pa_t_kernel(tc, hidden_states, cos, sin, w_qkv, out_0, out_1,
         for i in range(2, len(LOADS)):
             load_x(i)
 
-        out_of = {}
-        for (b, t0, n) in STORES:
-            q_sb = outp.tile([P, n, 2 * DH], F32, name="q%d_%d" % (b, t0))
-            k_sb = outp.tile([P, n, DH], F32, name="k%d_%d" % (b, t0))
-            v_sb = outp.tile([P, n, DH], F32, name="v%d_%d" % (b, t0))
-            for l0 in range(0, n, GT):
-                out_of[(b * TPB + t0 + l0) // GT] = (q_sb, k_sb, v_sb, l0, l0 + GT == n, b, t0, n)
+        outs = []
+        tiles = []
+        for c, (b, t0, n) in enumerate(BLOCKS):
+            q_sb = outp.tile([P, n, 2 * DH], F32, name="q%d" % c)
+            k_sb = outp.tile([P, n, DH], F32, name="k%d" % c)
+            v_sb = outp.tile([P, n, DH], F32, name="v%d" % c)
+            outs.append((q_sb, k_sb, v_sb))
+            for i in range(n):
+                tiles.append((c, i))
+        NT = len(tiles)
 
         iv = ident[:].rearrange("p (n e) -> p n e", e=2)
         pv = perm[:].rearrange("p (n e) -> p n e", e=2)
         nc.vector.tensor_copy(out=pv[:, :, 0], in_=iv[:, :, 1])
         nc.vector.tensor_copy(out=pv[:, :, 1], in_=iv[:, :, 0])
 
-        def evac(eng_is_vector, dst, bank):
+        def evac(on_vector, dst, bank):
             src = bank[:].rearrange("p a u r -> p a r u")
-            if eng_is_vector:
+            if on_vector:
                 nc.vector.tensor_copy(out=dst, in_=src)
             else:
                 nc.scalar.copy(out=dst, in_=src)
@@ -93,37 +94,37 @@ def tile_attention_pa_t_kernel(tc, hidden_states, cos, sin, w_qkv, out_0, out_1,
         mm_of = {}
         p_of = {}
 
-        def stage_t(g):
-            xt, l0 = x_of[g]
-            xw = xt[:].bitcast(F32)
+        def transposes(c):
+            b, t0, n = BLOCKS[c]
             banks = []
-            for h in range(2):
+            for h in range(n // 2):
                 tp = tpp.tile([P, 2, 2, P], F32, name="tp", tag="tp")
                 for a in range(2):
+                    xt, l = x_of[(b, t0 + 2 * h + a)]
+                    xw = xt[:].bitcast(F32)
                     for u in range(2):
-                        nc.tensor.transpose(tp[:, a, u, :], xw[:, l0 + 2 * h + a, P * u:P * (u + 1)], ident[:])
+                        nc.tensor.transpose(tp[:, a, u, :], xw[:, l, P * u:P * (u + 1)], ident[:])
                 banks.append(tp)
-            banks_of[g] = banks
+            banks_of[c] = banks
+            grp_of[c] = gp.tile([P, n, P, 4], BF16, name="grp", tag="grp", align_bytes=64)
 
-        def stage_e(g, second_on_vector=False):
-            grp = gp.tile([P, GT, P, 4], BF16, name="grp", tag="grp", align_bytes=64)
-            banks = banks_of[g]
-            evac(False, grp[:, 0:2].bitcast(F32), banks[0])
-            evac(second_on_vector, grp[:, 2:4].bitcast(F32), banks[1])
-            grp_of[g] = grp
+        def regroup(c, h, on_vector=False):
+            evac(on_vector, grp_of[c][:, 2 * h:2 * h + 2].bitcast(F32), banks_of[c][h])
 
-        def stage_q(g):
-            codes = cp.tile([P, GT * P], U32, name="codes", tag="codes", align_bytes=64)
-            scl = cp.tile([P, GT * P], U8, name="scl", tag="scl", align_bytes=64)
+        def quantise(c):
+            n = BLOCKS[c][2]
+            codes = cp.tile([P, n * P], U32, name="codes", tag="codes", align_bytes=64)
+            scl = cp.tile([P, n * P], U8, name="scl", tag="scl", align_bytes=64)
             nc.vector.quantize_mx(
                 out=codes[:].bitcast(FP8X4),
                 scales=scl[:],
-                in_=grp_of[g][:].rearrange("p a r t -> p (a r t)"),
+                in_=grp_of[c][:].rearrange("p a r t -> p (a r t)"),
             )
-            code_of[g] = (codes, scl)
+            code_of[c] = (codes, scl)
 
-        def stage_m(g, i):
-            codes, scl = code_of[g]
+        def project(m):
+            c, i = tiles[m]
+            codes, scl = code_of[c]
             mm = mmp.tile([P, 512], F32, name="mm", tag="mm")
             nc.tensor.matmul_mx(
                 out=mm[:],
@@ -134,32 +135,30 @@ def tile_attention_pa_t_kernel(tc, hidden_states, cos, sin, w_qkv, out_0, out_1,
                 start=True,
                 stop=True,
             )
-            mm_of[(g, i)] = mm
-            v_sb, l0 = out_of[g][2], out_of[g][3]
-            nc.scalar.copy(out=v_sb[:, l0 + i, :], in_=mm[:, 3 * DH:4 * DH])
+            mm_of[m] = mm
+            nc.scalar.copy(out=outs[c][2][:, i, :], in_=mm[:, 3 * DH:4 * DH])
 
-        def stage_x(g, i):
+        def multiply(m):
+            c, i = tiles[m]
+            b, t0, n = BLOCKS[c]
             if i == 0:
-                p_of[g] = pp.tile([P, GT, 2, 3 * DH], F32, name="prod", tag="prod")
-            t = (g * GT + i) % TPB
+                p_of[c] = pp.tile([P, n, 2, 3 * DH], F32, name="prod", tag="prod")
             nc.vector.tensor_tensor(
-                out=p_of[g][:, i].rearrange("p c (h j) -> p c h j", h=3),
-                in0=mm_of[(g, i)][:].rearrange("p (c h j) -> p c h j", c=2, h=4)[:, :, 0:3, :],
-                in1=tab[:, :, t, :].unsqueeze(2).to_broadcast([P, 2, 3, DH]),
+                out=p_of[c][:, i].rearrange("p c (h j) -> p c h j", h=3),
+                in0=mm_of[m][:].rearrange("p (c h j) -> p c h j", c=2, h=4)[:, :, 0:3, :],
+                in1=tab[:, :, t0 + i, :].unsqueeze(2).to_broadcast([P, 2, 3, DH]),
                 op=MULT,
             )
 
-        def stage_a(g):
-            q_sb, k_sb, v_sb, l0, last, b, t0, n = out_of[g]
-            prod = p_of[g]
-            eq = nc.vector if g in V_ADD_Q else nc.gpsimd
-            ek = nc.vector if g in V_ADD_K else nc.gpsimd
-            eq.tensor_tensor(out=q_sb[:, l0:l0 + GT, :], in0=prod[:, :, 0, 0:2 * DH], in1=prod[:, :, 1, 0:2 * DH], op=ADD)
-            ek.tensor_tensor(out=k_sb[:, l0:l0 + GT, :], in0=prod[:, :, 0, 2 * DH:3 * DH], in1=prod[:, :, 1, 2 * DH:3 * DH], op=ADD)
-            if last:
-                nc.sync.dma_start(out=out_2[b].rearrange("(p t) h j -> p t (h j)", t=TPB)[:, t0:t0 + n, :], in_=v_sb[:])
-                nc.sync.dma_start(out=out_0[b].rearrange("(p t) h j -> p t (h j)", t=TPB)[:, t0:t0 + n, :], in_=q_sb[:])
-                nc.sync.dma_start(out=out_1[b].rearrange("(p t) h j -> p t (h j)", t=TPB)[:, t0:t0 + n, :], in_=k_sb[:])
+        def add_and_store(c):
+            b, t0, n = BLOCKS[c]
+            q_sb, k_sb, v_sb = outs[c]
+            prod = p_of[c]
+            eng = nc.vector if c == NB - 1 else nc.gpsimd
+            eng.tensor_tensor(out=q_sb[:], in0=prod[:, :, 0, 0:2 * DH], in1=prod[:, :, 1, 0:2 * DH], op=ADD)
+            eng.tensor_tensor(out=k_sb[:], in0=prod[:, :, 0, 2 * DH:3 * DH], in1=prod[:, :, 1, 2 * DH:3 * DH], op=ADD)
+            for dram, sb in ((out_2, v_sb), (out_0, q_sb), (out_1, k_sb)):
+                nc.sync.dma_start(out=dram[b].rearrange("(p t) h j -> p t (h j)", t=TPB)[:, t0:t0 + n, :], in_=sb[:])
 
         ww = w_sb[:].bitcast(F32)
         w_grp = const.tile([P, 4, P, 4], BF16, name="w_grp", align_bytes=64)
@@ -174,32 +173,35 @@ def tile_attention_pa_t_kernel(tc, hidden_states, cos, sin, w_qkv, out_0, out_1,
             w_banks.append(tp)
         evac(False, w_grp[:, 0:2].bitcast(F32), w_banks[0])
         evac(True, w_grp[:, 2:4].bitcast(F32), w_banks[1])
-        stage_t(0)
+        transposes(0)
         nc.vector.quantize_mx(
             out=w_codes[:].bitcast(FP8X4),
             scales=w_scl[:],
             in_=w_grp[:].rearrange("p a r t -> p (a r t)"),
         )
-        stage_e(0, second_on_vector=True)
-        stage_t(1)
-        stage_q(0)
-        stage_e(1)
+        regroup(0, 0)
+        regroup(0, 1, on_vector=True)
+        transposes(1)
+        quantise(0)
+        regroup(1, 0)
+        regroup(1, 1)
         sv = tab[:, 1].rearrange("p t (i e) -> p (t i) e", e=2)[:, :, 0]
         nc.vector.tensor_scalar_mul(out=sv, in0=sv, scalar1=-1.0)
-        for i in range(GT):
-            stage_m(0, i)
-        stage_t(2)
-        stage_e(2)
+        for m in range(AHEAD):
+            project(m)
 
-        for k in range(NG):
-            if k + 3 < NG:
-                stage_t(k + 3)
-            if k + 1 < NG:
-                stage_q(k + 1)
-            if k + 3 < NG:
-                stage_e(k + 3)
-            for i in range(GT):
-                stage_x(k, i)
-                if k + 1 < NG:
-                    stage_m(k + 1, i)
-            stage_a(k)
+        m = 0
+        for c in range(NB):
+            n = BLOCKS[c][2]
+            if c + 2 < NB:
+                transposes(c + 2)
+            if c + 1 < NB:
+                quantise(c + 1)
+            for i in range(n):
+                multiply(m)
+                if m + AHEAD < NT:
+                    project(m + AHEAD)
+                if c + 2 < NB and i < BLOCKS[c + 2][2] // 2:
+                    regroup(c + 2, i)
+                m += 1
+            add_and_store(c)

@@ -15,12 +15,14 @@ P = 128
 B, S, HID = 4, 2048, 512
 DH = 64
 TPB = S // P
+GT = 4
+NG = B * TPB // GT
 FLOPS = 2 * B * S * HID * 256
 
 LOADS = [(0, 0, 4), (0, 4, 4), (0, 8, 8), (1, 0, 16), (2, 0, 16), (3, 0, 16)]
-BLOCKS = [(0, 0, 4), (0, 4, 4), (0, 8, 8), (1, 0, 8), (1, 8, 8), (2, 0, 8), (2, 8, 8), (3, 0, 8), (3, 8, 4), (3, 12, 4)]
-NB = len(BLOCKS)
-AHEAD = 4
+STORES = [(0, 0, 8), (0, 8, 8), (1, 0, 8), (1, 8, 8), (2, 0, 8), (2, 8, 8), (3, 0, 8), (3, 8, 4), (3, 12, 4)]
+V_ADD_Q = (15,)
+V_ADD_K = (1, 3, 5, 7, 9, 11, 13, 15)
 
 
 def tile_attention_pa_t_kernel(tc, hidden_states, cos, sin, w_qkv, out_0, out_1, out_2):
@@ -29,11 +31,11 @@ def tile_attention_pa_t_kernel(tc, hidden_states, cos, sin, w_qkv, out_0, out_1,
         const = ctx.enter_context(tc.tile_pool(name="const", bufs=1))
         xin = ctx.enter_context(tc.tile_pool(name="xin", bufs=1))
         outp = ctx.enter_context(tc.tile_pool(name="outp", bufs=1))
-        gp = ctx.enter_context(tc.tile_pool(name="gp", bufs=2))
+        gp = ctx.enter_context(tc.tile_pool(name="gp", bufs=3))
         cp = ctx.enter_context(tc.tile_pool(name="cp", bufs=2))
         pp = ctx.enter_context(tc.tile_pool(name="pp", bufs=3))
         tpp = ctx.enter_context(tc.psum_pool(name="tpp", bufs=4))
-        mmp = ctx.enter_context(tc.psum_pool(name="mmp", bufs=AHEAD))
+        mmp = ctx.enter_context(tc.psum_pool(name="mmp", bufs=4))
         ctx.enter_context(tc.manual_schedule())
 
         ident = const.tile([P, P], F32, name="ident")
@@ -48,8 +50,8 @@ def tile_attention_pa_t_kernel(tc, hidden_states, cos, sin, w_qkv, out_0, out_1,
         for (b, t0, n) in LOADS:
             xt = xin.tile([P, n, HID], BF16, name="x%d_%d" % (b, t0))
             x_tiles.append((xt, b, t0, n))
-            for l in range(n):
-                x_of[(b, t0 + l)] = (xt, l)
+            for l0 in range(0, n, GT):
+                x_of[(b * TPB + t0 + l0) // GT] = (xt, l0)
 
         def load_x(i):
             xt, b, t0, n = x_tiles[i]
@@ -65,25 +67,22 @@ def tile_attention_pa_t_kernel(tc, hidden_states, cos, sin, w_qkv, out_0, out_1,
         for i in range(2, len(LOADS)):
             load_x(i)
 
-        outs = []
-        tiles = []
-        for c, (b, t0, n) in enumerate(BLOCKS):
-            q_sb = outp.tile([P, n, 2 * DH], F32, name="q%d" % c)
-            k_sb = outp.tile([P, n, DH], F32, name="k%d" % c)
-            v_sb = outp.tile([P, n, DH], F32, name="v%d" % c)
-            outs.append((q_sb, k_sb, v_sb))
-            for i in range(n):
-                tiles.append((c, i))
-        NT = len(tiles)
+        out_of = {}
+        for (b, t0, n) in STORES:
+            q_sb = outp.tile([P, n, 2 * DH], F32, name="q%d_%d" % (b, t0))
+            k_sb = outp.tile([P, n, DH], F32, name="k%d_%d" % (b, t0))
+            v_sb = outp.tile([P, n, DH], F32, name="v%d_%d" % (b, t0))
+            for l0 in range(0, n, GT):
+                out_of[(b * TPB + t0 + l0) // GT] = (q_sb, k_sb, v_sb, l0, l0 + GT == n, b, t0, n)
 
         iv = ident[:].rearrange("p (n e) -> p n e", e=2)
         pv = perm[:].rearrange("p (n e) -> p n e", e=2)
         nc.vector.tensor_copy(out=pv[:, :, 0], in_=iv[:, :, 1])
         nc.vector.tensor_copy(out=pv[:, :, 1], in_=iv[:, :, 0])
 
-        def evac(on_vector, dst, bank):
+        def evac(eng_is_vector, dst, bank):
             src = bank[:].rearrange("p a u r -> p a r u")
-            if on_vector:
+            if eng_is_vector:
                 nc.vector.tensor_copy(out=dst, in_=src)
             else:
                 nc.scalar.copy(out=dst, in_=src)
@@ -94,37 +93,37 @@ def tile_attention_pa_t_kernel(tc, hidden_states, cos, sin, w_qkv, out_0, out_1,
         mm_of = {}
         p_of = {}
 
-        def transposes(c):
-            b, t0, n = BLOCKS[c]
+        def stage_t(g):
+            xt, l0 = x_of[g]
+            xw = xt[:].bitcast(F32)
             banks = []
-            for h in range(n // 2):
+            for h in range(2):
                 tp = tpp.tile([P, 2, 2, P], F32, name="tp", tag="tp")
                 for a in range(2):
-                    xt, l = x_of[(b, t0 + 2 * h + a)]
-                    xw = xt[:].bitcast(F32)
                     for u in range(2):
-                        nc.tensor.transpose(tp[:, a, u, :], xw[:, l, P * u:P * (u + 1)], ident[:])
+                        nc.tensor.transpose(tp[:, a, u, :], xw[:, l0 + 2 * h + a, P * u:P * (u + 1)], ident[:])
                 banks.append(tp)
-            banks_of[c] = banks
-            grp_of[c] = gp.tile([P, n, P, 4], BF16, name="grp", tag="grp", align_bytes=64)
+            banks_of[g] = banks
 
-        def regroup(c, h, on_vector=False):
-            evac(on_vector, grp_of[c][:, 2 * h:2 * h + 2].bitcast(F32), banks_of[c][h])
+        def stage_e(g, second_on_vector=False):
+            grp = gp.tile([P, GT, P, 4], BF16, name="grp", tag="grp", align_bytes=64)
+            banks = banks_of[g]
+            evac(False, grp[:, 0:2].bitcast(F32), banks[0])
+            evac(second_on_vector, grp[:, 2:4].bitcast(F32), banks[1])
+            grp_of[g] = grp
 
-        def quantise(c):
-            n = BLOCKS[c][2]
-            codes = cp.tile([P, n * P], U32, name="codes", tag="codes", align_bytes=64)
-            scl = cp.tile([P, n * P], U8, name="scl", tag="scl", align_bytes=64)
+        def stage_q(g):
+            codes = cp.tile([P, GT * P], U32, name="codes", tag="codes", align_bytes=64)
+            scl = cp.tile([P, GT * P], U8, name="scl", tag="scl", align_bytes=64)
             nc.vector.quantize_mx(
                 out=codes[:].bitcast(FP8X4),
                 scales=scl[:],
-                in_=grp_of[c][:].rearrange("p a r t -> p (a r t)"),
+                in_=grp_of[g][:].rearrange("p a r t -> p (a r t)"),
             )
-            code_of[c] = (codes, scl)
+            code_of[g] = (codes, scl)
 
-        def project(m):
-            c, i = tiles[m]
-            codes, scl = code_of[c]
+        def stage_m(g, i):
+            codes, scl = code_of[g]
             mm = mmp.tile([P, 512], F32, name="mm", tag="mm")
             nc.tensor.matmul_mx(
                 out=mm[:],
@@ -135,30 +134,32 @@ def tile_attention_pa_t_kernel(tc, hidden_states, cos, sin, w_qkv, out_0, out_1,
                 start=True,
                 stop=True,
             )
-            mm_of[m] = mm
-            nc.scalar.copy(out=outs[c][2][:, i, :], in_=mm[:, 3 * DH:4 * DH])
+            mm_of[(g, i)] = mm
+            v_sb, l0 = out_of[g][2], out_of[g][3]
+            nc.scalar.copy(out=v_sb[:, l0 + i, :], in_=mm[:, 3 * DH:4 * DH])
 
-        def multiply(m):
-            c, i = tiles[m]
-            b, t0, n = BLOCKS[c]
+        def stage_x(g, i):
             if i == 0:
-                p_of[c] = pp.tile([P, n, 2, 3 * DH], F32, name="prod", tag="prod")
+                p_of[g] = pp.tile([P, GT, 2, 3 * DH], F32, name="prod", tag="prod")
+            t = (g * GT + i) % TPB
             nc.vector.tensor_tensor(
-                out=p_of[c][:, i].rearrange("p c (h j) -> p c h j", h=3),
-                in0=mm_of[m][:].rearrange("p (c h j) -> p c h j", c=2, h=4)[:, :, 0:3, :],
-                in1=tab[:, :, t0 + i, :].unsqueeze(2).to_broadcast([P, 2, 3, DH]),
+                out=p_of[g][:, i].rearrange("p c (h j) -> p c h j", h=3),
+                in0=mm_of[(g, i)][:].rearrange("p (c h j) -> p c h j", c=2, h=4)[:, :, 0:3, :],
+                in1=tab[:, :, t, :].unsqueeze(2).to_broadcast([P, 2, 3, DH]),
                 op=MULT,
             )
 
-        def add_and_store(c):
-            b, t0, n = BLOCKS[c]
-            q_sb, k_sb, v_sb = outs[c]
-            prod = p_of[c]
-            eng = nc.vector if c == NB - 1 else nc.gpsimd
-            eng.tensor_tensor(out=q_sb[:], in0=prod[:, :, 0, 0:2 * DH], in1=prod[:, :, 1, 0:2 * DH], op=ADD)
-            eng.tensor_tensor(out=k_sb[:], in0=prod[:, :, 0, 2 * DH:3 * DH], in1=prod[:, :, 1, 2 * DH:3 * DH], op=ADD)
-            for dram, sb in ((out_2, v_sb), (out_0, q_sb), (out_1, k_sb)):
-                nc.sync.dma_start(out=dram[b].rearrange("(p t) h j -> p t (h j)", t=TPB)[:, t0:t0 + n, :], in_=sb[:])
+        def stage_a(g):
+            q_sb, k_sb, v_sb, l0, last, b, t0, n = out_of[g]
+            prod = p_of[g]
+            eq = nc.vector if g in V_ADD_Q else nc.gpsimd
+            ek = nc.vector if g in V_ADD_K else nc.gpsimd
+            eq.tensor_tensor(out=q_sb[:, l0:l0 + GT, :], in0=prod[:, :, 0, 0:2 * DH], in1=prod[:, :, 1, 0:2 * DH], op=ADD)
+            ek.tensor_tensor(out=k_sb[:, l0:l0 + GT, :], in0=prod[:, :, 0, 2 * DH:3 * DH], in1=prod[:, :, 1, 2 * DH:3 * DH], op=ADD)
+            if last:
+                nc.sync.dma_start(out=out_2[b].rearrange("(p t) h j -> p t (h j)", t=TPB)[:, t0:t0 + n, :], in_=v_sb[:])
+                nc.sync.dma_start(out=out_0[b].rearrange("(p t) h j -> p t (h j)", t=TPB)[:, t0:t0 + n, :], in_=q_sb[:])
+                nc.sync.dma_start(out=out_1[b].rearrange("(p t) h j -> p t (h j)", t=TPB)[:, t0:t0 + n, :], in_=k_sb[:])
 
         ww = w_sb[:].bitcast(F32)
         w_grp = const.tile([P, 4, P, 4], BF16, name="w_grp", align_bytes=64)
@@ -173,35 +174,32 @@ def tile_attention_pa_t_kernel(tc, hidden_states, cos, sin, w_qkv, out_0, out_1,
             w_banks.append(tp)
         evac(False, w_grp[:, 0:2].bitcast(F32), w_banks[0])
         evac(True, w_grp[:, 2:4].bitcast(F32), w_banks[1])
-        transposes(0)
+        stage_t(0)
         nc.vector.quantize_mx(
             out=w_codes[:].bitcast(FP8X4),
             scales=w_scl[:],
             in_=w_grp[:].rearrange("p a r t -> p (a r t)"),
         )
-        regroup(0, 0)
-        regroup(0, 1, on_vector=True)
-        transposes(1)
-        quantise(0)
-        regroup(1, 0)
-        regroup(1, 1)
+        stage_e(0, second_on_vector=True)
+        stage_t(1)
+        stage_q(0)
+        stage_e(1)
         sv = tab[:, 1].rearrange("p t (i e) -> p (t i) e", e=2)[:, :, 0]
         nc.vector.tensor_scalar_mul(out=sv, in0=sv, scalar1=-1.0)
-        for m in range(AHEAD):
-            project(m)
+        for i in range(GT):
+            stage_m(0, i)
+        stage_t(2)
+        stage_e(2)
 
-        m = 0
-        for c in range(NB):
-            n = BLOCKS[c][2]
-            if c + 2 < NB:
-                transposes(c + 2)
-            if c + 1 < NB:
-                quantise(c + 1)
-            for i in range(n):
-                multiply(m)
-                if m + AHEAD < NT:
-                    project(m + AHEAD)
-                if c + 2 < NB and i < BLOCKS[c + 2][2] // 2:
-                    regroup(c + 2, i)
-                m += 1
-            add_and_store(c)
+        for k in range(NG):
+            if k + 3 < NG:
+                stage_t(k + 3)
+            if k + 1 < NG:
+                stage_q(k + 1)
+            if k + 3 < NG:
+                stage_e(k + 3)
+            for i in range(GT):
+                stage_x(k, i)
+                if k + 1 < NG:
+                    stage_m(k + 1, i)
+            stage_a(k)

@@ -22,7 +22,7 @@ FLOPS = 2 * B * S * HID * 256
 LOADS = [(0, 0, 4), (0, 4, 4), (0, 8, 8), (1, 0, 16), (2, 0, 16), (3, 0, 16)]
 STORES = [(0, 0, 8), (0, 8, 8), (1, 0, 8), (1, 8, 8), (2, 0, 8), (2, 8, 8), (3, 0, 8), (3, 8, 4), (3, 12, 4)]
 V_ADD_Q = (15,)
-V_ADD_K = (1, 3, 5, 7, 9, 11, 13, 15)
+V_ADD_K = (3, 7, 11, 14, 15)
 
 
 def tile_attention_pa_t_kernel(tc, hidden_states, cos, sin, w_qkv, out_0, out_1, out_2):

from contextlib import ExitStack

import concourse.mybir as mybir
from concourse.masks import make_identity

F32 = mybir.dt.float32
BF16 = mybir.dt.bfloat16
U32 = mybir.dt.uint32
U8 = mybir.dt.uint8
FP8X4 = mybir.dt.float8_e4m3fn_x4
MULT = mybir.AluOpType.mult
ADD = mybir.AluOpType.add

P = 128
B, S, HID = 4, 2048, 512
DH = 64
TPB = S // P
GT = 4
NG = B * TPB // GT
FLOPS = 2 * B * S * HID * 256

LOADS = [(0, 0, 4), (0, 4, 4), (0, 8, 8), (1, 0, 16), (2, 0, 16), (3, 0, 16)]
STORES = [(0, 0, 8), (0, 8, 8), (1, 0, 8), (1, 8, 8), (2, 0, 8), (2, 8, 8), (3, 0, 8), (3, 8, 4), (3, 12, 4)]
V_ADD_Q = (15,)
V_ADD_K = (3, 7, 11, 14, 15)


def tile_attention_pa_t_kernel(tc, hidden_states, cos, sin, w_qkv, out_0, out_1, out_2):
    nc = tc.nc
    with ExitStack() as ctx:
        const = ctx.enter_context(tc.tile_pool(name="const", bufs=1))
        xin = ctx.enter_context(tc.tile_pool(name="xin", bufs=1))
        outp = ctx.enter_context(tc.tile_pool(name="outp", bufs=1))
        gp = ctx.enter_context(tc.tile_pool(name="gp", bufs=3))
        cp = ctx.enter_context(tc.tile_pool(name="cp", bufs=2))
        pp = ctx.enter_context(tc.tile_pool(name="pp", bufs=3))
        tpp = ctx.enter_context(tc.psum_pool(name="tpp", bufs=4))
        mmp = ctx.enter_context(tc.psum_pool(name="mmp", bufs=4))
        ctx.enter_context(tc.manual_schedule())

        ident = const.tile([P, P], F32, name="ident")
        make_identity(nc, ident[:])
        perm = const.tile([P, P], F32, name="perm")
        w_sb = const.tile([P, 2, HID], BF16, name="w_sb")
        tab = const.tile([P, 2, TPB, DH], BF16, name="tab")

        nc.sync.dma_start(out=w_sb[:], in_=w_qkv.rearrange("(a p) k -> p a k", p=P))
        x_of = {}
        x_tiles = []
        for (b, t0, n) in LOADS:
            xt = xin.tile([P, n, HID], BF16, name="x%d_%d" % (b, t0))
            x_tiles.append((xt, b, t0, n))
            for l0 in range(0, n, GT):
                x_of[(b * TPB + t0 + l0) // GT] = (xt, l0)

        def load_x(i):
            xt, b, t0, n = x_tiles[i]
            nc.sync.dma_start(
                out=xt[:],
                in_=hidden_states[b].rearrange("(p t) k -> p t k", t=TPB)[:, t0:t0 + n, :],
            )

        load_x(0)
        load_x(1)
        nc.sync.dma_start(out=tab[:, 1], in_=sin.rearrange("(p t) j -> p t j", t=TPB))
        nc.sync.dma_start(out=tab[:, 0], in_=cos.rearrange("(p t) j -> p t j", t=TPB))
        for i in range(2, len(LOADS)):
            load_x(i)

        out_of = {}
        for (b, t0, n) in STORES:
            q_sb = outp.tile([P, n, 2 * DH], F32, name="q%d_%d" % (b, t0))
            k_sb = outp.tile([P, n, DH], F32, name="k%d_%d" % (b, t0))
            v_sb = outp.tile([P, n, DH], F32, name="v%d_%d" % (b, t0))
            for l0 in range(0, n, GT):
                out_of[(b * TPB + t0 + l0) // GT] = (q_sb, k_sb, v_sb, l0, l0 + GT == n, b, t0, n)

        iv = ident[:].rearrange("p (n e) -> p n e", e=2)
        pv = perm[:].rearrange("p (n e) -> p n e", e=2)
        nc.vector.tensor_copy(out=pv[:, :, 0], in_=iv[:, :, 1])
        nc.vector.tensor_copy(out=pv[:, :, 1], in_=iv[:, :, 0])

        def evac(eng_is_vector, dst, bank):
            src = bank[:].rearrange("p a u r -> p a r u")
            if eng_is_vector:
                nc.vector.tensor_copy(out=dst, in_=src)
            else:
                nc.scalar.copy(out=dst, in_=src)

        banks_of = {}
        grp_of = {}
        code_of = {}
        mm_of = {}
        p_of = {}

        def stage_t(g):
            xt, l0 = x_of[g]
            xw = xt[:].bitcast(F32)
            banks = []
            for h in range(2):
                tp = tpp.tile([P, 2, 2, P], F32, name="tp", tag="tp")
                for a in range(2):
                    for u in range(2):
                        nc.tensor.transpose(tp[:, a, u, :], xw[:, l0 + 2 * h + a, P * u:P * (u + 1)], ident[:])
                banks.append(tp)
            banks_of[g] = banks

        def stage_e(g, second_on_vector=False):
            grp = gp.tile([P, GT, P, 4], BF16, name="grp", tag="grp", align_bytes=64)
            banks = banks_of[g]
            evac(False, grp[:, 0:2].bitcast(F32), banks[0])
            evac(second_on_vector, grp[:, 2:4].bitcast(F32), banks[1])
            grp_of[g] = grp

        def stage_q(g):
            codes = cp.tile([P, GT * P], U32, name="codes", tag="codes", align_bytes=64)
            scl = cp.tile([P, GT * P], U8, name="scl", tag="scl", align_bytes=64)
            nc.vector.quantize_mx(
                out=codes[:].bitcast(FP8X4),
                scales=scl[:],
                in_=grp_of[g][:].rearrange("p a r t -> p (a r t)"),
            )
            code_of[g] = (codes, scl)

        def stage_m(g, i):
            codes, scl = code_of[g]
            mm = mmp.tile([P, 512], F32, name="mm", tag="mm")
            nc.tensor.matmul_mx(
                out=mm[:],
                lhsT=codes[:, P * i:P * (i + 1)].bitcast(FP8X4),
                lhsT_scale=scl[:, P * i:P * (i + 1)],
                rhs=w_codes[:].bitcast(FP8X4),
                rhs_scale=w_scl[:],
                start=True,
                stop=True,
            )
            mm_of[(g, i)] = mm
            v_sb, l0 = out_of[g][2], out_of[g][3]
            nc.scalar.copy(out=v_sb[:, l0 + i, :], in_=mm[:, 3 * DH:4 * DH])

        def stage_x(g, i):
            if i == 0:
                p_of[g] = pp.tile([P, GT, 2, 3 * DH], F32, name="prod", tag="prod")
            t = (g * GT + i) % TPB
            nc.vector.tensor_tensor(
                out=p_of[g][:, i].rearrange("p c (h j) -> p c h j", h=3),
                in0=mm_of[(g, i)][:].rearrange("p (c h j) -> p c h j", c=2, h=4)[:, :, 0:3, :],
                in1=tab[:, :, t, :].unsqueeze(2).to_broadcast([P, 2, 3, DH]),
                op=MULT,
            )

        def stage_a(g):
            q_sb, k_sb, v_sb, l0, last, b, t0, n = out_of[g]
            prod = p_of[g]
            eq = nc.vector if g in V_ADD_Q else nc.gpsimd
            ek = nc.vector if g in V_ADD_K else nc.gpsimd
            eq.tensor_tensor(out=q_sb[:, l0:l0 + GT, :], in0=prod[:, :, 0, 0:2 * DH], in1=prod[:, :, 1, 0:2 * DH], op=ADD)
            ek.tensor_tensor(out=k_sb[:, l0:l0 + GT, :], in0=prod[:, :, 0, 2 * DH:3 * DH], in1=prod[:, :, 1, 2 * DH:3 * DH], op=ADD)
            if last:
                nc.sync.dma_start(out=out_2[b].rearrange("(p t) h j -> p t (h j)", t=TPB)[:, t0:t0 + n, :], in_=v_sb[:])
                nc.sync.dma_start(out=out_0[b].rearrange("(p t) h j -> p t (h j)", t=TPB)[:, t0:t0 + n, :], in_=q_sb[:])
                nc.sync.dma_start(out=out_1[b].rearrange("(p t) h j -> p t (h j)", t=TPB)[:, t0:t0 + n, :], in_=k_sb[:])

        ww = w_sb[:].bitcast(F32)
        w_grp = const.tile([P, 4, P, 4], BF16, name="w_grp", align_bytes=64)
        w_codes = const.tile([P, 512], U32, name="w_codes", align_bytes=64)
        w_scl = const.tile([P, 512], U8, name="w_scl", align_bytes=64)
        w_banks = []
        for mat in (ident, perm):
            tp = tpp.tile([P, 2, 2, P], F32, name="tp", tag="tp")
            for a in range(2):
                for u in range(2):
                    nc.tensor.transpose(tp[:, a, u, :], ww[:, a, P * u:P * (u + 1)], mat[:])
            w_banks.append(tp)
        evac(False, w_grp[:, 0:2].bitcast(F32), w_banks[0])
        evac(True, w_grp[:, 2:4].bitcast(F32), w_banks[1])
        stage_t(0)
        nc.vector.quantize_mx(
            out=w_codes[:].bitcast(FP8X4),
            scales=w_scl[:],
            in_=w_grp[:].rearrange("p a r t -> p (a r t)"),
        )
        stage_e(0, second_on_vector=True)
        stage_t(1)
        stage_q(0)
        stage_e(1)
        sv = tab[:, 1].rearrange("p t (i e) -> p (t i) e", e=2)[:, :, 0]
        nc.vector.tensor_scalar_mul(out=sv, in0=sv, scalar1=-1.0)
        for i in range(GT):
            stage_m(0, i)
        stage_t(2)
        stage_e(2)

        for k in range(NG):
            if k + 3 < NG:
                stage_t(k + 3)
            if k + 1 < NG:
                stage_q(k + 1)
            if k + 3 < NG:
                stage_e(k + 3)
            for i in range(GT):
                stage_x(k, i)
                if k + 1 < NG:
                    stage_m(k + 1, i)
            stage_a(k)
